import numpy as np
import ml_dtypes


def mxq(x, axis, fmt="e4m3"):
    dtype, down = {"e4m3": (ml_dtypes.float8_e4m3fn, 7), "e5m2": (ml_dtypes.float8_e5m2, 14)}[fmt]
    v = np.moveaxis(np.asarray(x, np.float32).astype(ml_dtypes.bfloat16).astype(np.float64), axis, -1)
    blocks = v.reshape(v.shape[:-1] + (-1, 32))
    amax = np.abs(blocks).max(-1, keepdims=True)
    byte = np.maximum(np.where(amax > 0, np.frexp(amax)[1] - 1 + 127, 0) - down, 1)
    scale = np.exp2(byte - 127.0)
    codes = (blocks / scale).astype(np.float32).astype(dtype).astype(np.float64)
    return np.moveaxis((codes * scale).reshape(v.shape), -1, axis)


WIDE = False


def mx_kscale(k):
    if not WIDE:
        return np.ones(k)
    levels = np.array([10, -10, 5, -5, 0])
    a = np.random.permutation(np.resize(levels, k // 512 * 4)).reshape(k // 512, 4)
    idx = np.arange(k)
    return np.exp2(a[idx // 512, idx % 128 // 32])


BF16 = ml_dtypes.bfloat16


def bf(x):
    return np.asarray(x, np.float32).astype(BF16)


def f64(x):
    return np.asarray(x).astype(np.float64)


B, H, W, C, F, K, G, RR = 2, 16, 16, 16384, 256, 3, 16, 4
KK = K * K
P = B * H * W


def setup_inputs():
    s = mx_kscale(C)
    return {"x": bf(np.random.standard_normal((B, H, W, C)) * s),
            "Wi": bf(np.random.standard_normal((C, F)) / np.sqrt(C) / s[:, None]),
            "bi": bf(np.random.standard_normal(F) * 0.3),
            "w_span": bf(np.random.standard_normal((B, H, W, KK * G)) * 0.7)}


def reference(x, Wi, bi, w_span):
    xi = ((mxq(f64(x).reshape(P, C), 1, "e4m3") @ mxq(f64(Wi), 0, "e4m3")) + f64(bi)).reshape(B, H, W, F)
    pad = (K - 1) // 2
    xp = np.pad(xi, ((0, 0), (pad, pad), (pad, pad), (0, 0)))
    patches = np.stack([xp[:, i:i + H, j:j + W, :] for i in range(K) for j in range(K)], axis=-2)
    patches = patches.reshape(B, H, W, G, F // G, KK)
    w = f64(w_span).reshape(B, H, W, G, KK)[:, :, :, :, None, :]
    return (w * patches).sum(-1).reshape(B, H, W, F)

@@ -1,0 +1,275 @@
+from contextlib import ExitStack
+
+import concourse.mybir as mybir
+from concourse.masks import make_identity
+
+F32 = mybir.dt.float32
+BF16 = mybir.dt.bfloat16
+U32 = mybir.dt.uint32
+U8 = mybir.dt.uint8
+FP8X4 = mybir.dt.float8_e4m3fn_x4
+ALU = mybir.AluOpType
+ACT = mybir.ActivationFunctionType
+AXIS = mybir.AxisListType
+
+P = 128
+IMAGES = 2
+SIDE = 16
+IMG_PIX = SIDE * SIDE
+HALVES = IMG_PIX // P
+C_IN = 16384
+F_OUT = 256
+F_TILES = F_OUT // P
+PACK = 4
+K_PASS = P * PACK
+PASS_WORDS = K_PASS // 2
+PASSES = C_IN // K_PASS
+ROUND = 4
+ROUNDS = PASSES // ROUND
+CHUNK_ROUNDS = 2
+CHUNK_K = CHUNK_ROUNDS * ROUND * K_PASS
+LOAD_AHEAD = 4
+
+TAPS = 9
+GROUPS = 16
+GROUP_CH = F_OUT // GROUPS
+WIN_GROUPS = 2
+WIN = WIN_GROUPS * GROUP_CH * TAPS
+WINDOWS = GROUPS // WIN_GROUPS
+WIN_BLOCKS = 3
+XI_LEFT = 32
+XI_WIDTH = 320
+
+FLOPS = 2 * IMAGES * IMG_PIX * C_IN * F_OUT
+
+
+def tile_involution2d_pa_k_kernel(tc, x, Wi, bi, w_span, out):
+    nc = tc.nc
+    x_rows = x.rearrange("b u v k -> (b u v) k")
+    out_rows = out.rearrange("b u v o -> (b u v) o")
+    wi_rows = Wi.rearrange("(a p e) c -> p a (e c)", p=P, e=2)
+
+    with ExitStack() as ctx:
+        const = ctx.enter_context(tc.tile_pool(name="const", bufs=1))
+        x_pool = ctx.enter_context(tc.tile_pool(name="x_pool", bufs=3))
+        wi_raw_pool = ctx.enter_context(tc.tile_pool(name="wi_raw_pool", bufs=LOAD_AHEAD + 1))
+        wi_grp_pool = ctx.enter_context(tc.tile_pool(name="wi_grp_pool", bufs=2))
+        x_grp_pool = ctx.enter_context(tc.tile_pool(name="x_grp_pool", bufs=3))
+        x_mx_pool = ctx.enter_context(tc.tile_pool(name="x_mx_pool", bufs=3))
+        tail_pool = ctx.enter_context(tc.tile_pool(name="tail_pool", bufs=2))
+        acc_pool = ctx.enter_context(tc.psum_pool(name="acc_pool", bufs=1))
+        xt_pool = ctx.enter_context(tc.psum_pool(name="xt_pool", bufs=4))
+        patch_pool = ctx.enter_context(tc.psum_pool(name="patch_pool", bufs=2))
+
+        ident = const.tile([P, P], F32)
+        make_identity(nc, ident[:])
+
+        w_sb = const.tile([P, IMAGES * HALVES, GROUPS * TAPS], BF16)
+        nc.scalar.dma_start(
+            out=w_sb[:],
+            in_=w_span.rearrange("b u v q -> (b u v) q").rearrange("(r p) q -> p r q", p=P),
+        )
+
+        bias_rows = const.tile([P, P], BF16)
+        nc.vector.memset(bias_rows[:], 0.0)
+        nc.scalar.dma_start(out=bias_rows[0:F_TILES, :], in_=bi.rearrange("(f c) -> f c", f=F_TILES))
+        bias_rows32 = const.tile([P, P], F32)
+        nc.vector.tensor_copy(out=bias_rows32[:], in_=bias_rows[:])
+        patch = patch_pool.tile([P, WIN_BLOCKS * P], F32)
+        nc.tensor.transpose(patch[:, 0:P], bias_rows32[:], ident[:])
+        bias_col = const.tile([P, F_TILES], F32)
+        nc.vector.tensor_copy(out=bias_col[:], in_=patch[:, 0:F_TILES])
+
+        xi_copies = []
+        for b in range(IMAGES):
+            xi = const.tile([P, 3, F_TILES, XI_WIDTH], F32, name="xi%d" % b)
+            nc.vector.memset(xi[:], 0.0)
+            xi_copies.append(xi)
+
+        wi_codes = const.tile([P, PASSES * F_OUT], U32, align_bytes=64)
+        wi_scales = const.tile([P, PASSES * F_OUT], U8, align_bytes=64)
+
+        wi_raw = {}
+        x_chunks = {}
+
+        def issue_loads(step):
+            if step % CHUNK_ROUNDS == 0:
+                chunk = step // CHUNK_ROUNDS
+                b, part = divmod(chunk, ROUNDS // CHUNK_ROUNDS)
+                x_chunk = x_pool.tile([P, HALVES, CHUNK_K], BF16)
+                for h in range(HALVES):
+                    first_pixel = (b * HALVES + h) * P
+                    nc.sync.dma_start(
+                        out=x_chunk[:, h, :],
+                        in_=x_rows[first_pixel : first_pixel + P, part * CHUNK_K : (part + 1) * CHUNK_K],
+                    )
+                x_chunks[chunk] = x_chunk
+            if step < ROUNDS:
+                raw = wi_raw_pool.tile([P, ROUND, PACK, F_OUT], BF16)
+                nc.sync.dma_start(
+                    out=raw[:].rearrange("p g (u e) c -> p (g u) (e c)", u=2),
+                    in_=wi_rows[:, 2 * ROUND * step : 2 * ROUND * (step + 1), :],
+                )
+                wi_raw[step] = raw
+
+        def regroup_wi(kr):
+            raw = wi_raw[kr]
+            grouped = wi_grp_pool.tile([P, ROUND, F_OUT, PACK], BF16, align_bytes=64)
+            for g in range(ROUND):
+                dst = grouped[:, g, :, :].rearrange("p (c i) t -> p c t i", i=4)
+                src = raw[:, g, :, :].rearrange("p t (c i) -> p c t i", i=4)
+                if g % 2 == 0:
+                    nc.vector.tensor_copy(out=dst, in_=src)
+                else:
+                    nc.scalar.copy(out=dst, in_=src)
+            return grouped
+
+        def quantise_wi(kr, grouped):
+            cols = slice(kr * ROUND * F_OUT, (kr + 1) * ROUND * F_OUT)
+            nc.vector.quantize_mx(
+                out=wi_codes[:, cols].bitcast(FP8X4),
+                scales=wi_scales[:, cols],
+                in_=grouped[:].rearrange("p g c t -> p (g c t)"),
+            )
+
+        def transpose_x(step):
+            x_chunk = x_chunks[step // CHUNK_ROUNDS]
+            grouped = x_grp_pool.tile([P, ROUND * IMG_PIX * PACK], BF16, align_bytes=64)
+            grouped_words = grouped[:].bitcast(F32)
+            for g in range(ROUND):
+                first_word = ((step % CHUNK_ROUNDS) * ROUND + g) * PASS_WORDS
+                bank = xt_pool.tile([P, 2, IMG_PIX], F32)
+                for u in range(2):
+                    for h in range(HALVES):
+                        nc.tensor.transpose(
+                            bank[:, u, h * P : (h + 1) * P],
+                            x_chunk[:, h, :].bitcast(F32)[:, first_word + u * P : first_word + (u + 1) * P],
+                            ident[:],
+                        )
+                nc.scalar.copy(
+                    out=grouped_words[:, g * 2 * IMG_PIX : (g + 1) * 2 * IMG_PIX].rearrange(
+                        "p (r u) -> p r u", u=2
+                    ),
+                    in_=bank[:].rearrange("p u r -> p r u"),
+                )
+            return grouped
+
+        def quantise_x(grouped):
+            codes = x_mx_pool.tile([P, ROUND * IMG_PIX], U32, align_bytes=64)
+            scales = x_mx_pool.tile([P, ROUND * IMG_PIX], U8, align_bytes=64)
+            nc.vector.quantize_mx(out=codes[:].bitcast(FP8X4), scales=scales[:], in_=grouped[:])
+            return codes, scales
+
+        def multiply(kr, acc, codes, scales):
+            for g in range(ROUND):
+                k_pass = kr * ROUND + g
+                pixels = slice(g * IMG_PIX, (g + 1) * IMG_PIX)
+                for f in range(F_TILES):
+                    columns = slice(k_pass * F_OUT + f * P, k_pass * F_OUT + (f + 1) * P)
+                    nc.tensor.matmul_mx(
+                        out=acc[f][:],
+                        lhsT=wi_codes[:, columns].bitcast(FP8X4),
+                        lhsT_scale=wi_scales[:, columns],
+                        rhs=codes[:, pixels].bitcast(FP8X4),
+                        rhs_scale=scales[:, pixels],
+                        start=(k_pass == 0),
+                        stop=(k_pass == PASSES - 1),
+                    )
+
+        def spread_xi(b, acc):
+            xi = xi_copies[b]
+            for f in range(F_TILES):
+                image = acc[f][:].rearrange("p (u v) -> p u v", v=SIDE)
+                for j in range(3):
+                    v_lo = max(0, j - 1)
+                    v_hi = min(SIDE, SIDE - 1 + j)
+                    first = XI_LEFT - (j - 1)
+                    dst = xi[:, j, f, first : first + IMG_PIX].rearrange("p (u v) -> p u v", v=SIDE)
+                    if f == 0:
+                        nc.scalar.activation(
+                            out=dst[:, :, v_lo:v_hi],
+                            in_=image[:, :, v_lo:v_hi],
+                            func=ACT.Identity,
+                            bias=bias_col[:, f : f + 1],
+                            scale=1.0,
+                        )
+                    else:
+                        nc.vector.tensor_scalar(
+                            out=dst[:, :, v_lo:v_hi],
+                            in0=image[:, :, v_lo:v_hi],
+                            scalar1=bias_col[:, f : f + 1],
+                            scalar2=None,
+                            op0=ALU.add,
+                        )
+
+        def weigh_window(b, h, wd, products):
+            xi = xi_copies[b]
+            first_block = (WIN * wd) // P
+            skip = WIN * wd - first_block * P
+            patch = patch_pool.tile([P, WIN_BLOCKS * P], F32)
+            for s in range(WIN_BLOCKS):
+                t, f = divmod(first_block + s, F_TILES)
+                i, j = divmod(t, 3)
+                start = XI_LEFT + h * P + (i - 1) * SIDE
+                nc.tensor.transpose(patch[:, s * P : (s + 1) * P], xi[:, j, f, start : start + P], ident[:])
+            weights = w_sb[:, b * HALVES + h, WIN_GROUPS * TAPS * wd : WIN_GROUPS * TAPS * (wd + 1)]
+            nc.vector.tensor_tensor(
+                out=products[:, WIN * wd : WIN * (wd + 1)].rearrange("p (g c m) -> p g c m", g=WIN_GROUPS, m=TAPS),
+                in0=patch[:, skip : skip + WIN].rearrange("p (g c m) -> p g c m", g=WIN_GROUPS, m=TAPS),
+                in1=weights.rearrange("p (g m) -> p g m", m=TAPS)
+                .unsqueeze(2)
+                .to_broadcast([P, WIN_GROUPS, GROUP_CH, TAPS]),
+                op=ALU.mult,
+            )
+
+        def sum_and_store(b, h, products):
+            result = tail_pool.tile([P, F_OUT], F32)
+            nc.vector.tensor_reduce(
+                out=result[:],
+                in_=products[:].rearrange("p (o m) -> p o m", m=TAPS),
+                axis=AXIS.X,
+                op=ALU.add,
+            )
+            first_pixel = (b * HALVES + h) * P
+            nc.sync.dma_start(out=out_rows[first_pixel : first_pixel + P, :], in_=result[:])
+
+        products_of = {}
+
+        def involution_windows(b, first, count):
+            for e in range(first, first + count):
+                h, wd = divmod(e, WINDOWS)
+                if wd == 0:
+                    products = tail_pool.tile([P, F_OUT * TAPS], F32)
+                    products_of[h] = products
+                weigh_window(b, h, wd, products_of[h])
+                if wd == WINDOWS - 1:
+                    sum_and_store(b, h, products_of[h])
+
+        steps = IMAGES * ROUNDS
+        windows_per_step = HALVES * WINDOWS // ROUNDS
+        for step in range(LOAD_AHEAD):
+            issue_loads(step)
+        wi_grouped = regroup_wi(0)
+        x_grouped = transpose_x(0)
+        quantise_wi(0, wi_grouped)
+        acc = None
+        for step in range(steps):
+            b, kr = divmod(step, ROUNDS)
+            if step + LOAD_AHEAD < steps:
+                issue_loads(step + LOAD_AHEAD)
+            if kr == 0:
+                acc = [acc_pool.tile([P, IMG_PIX], F32, name="acc%d" % f) for f in range(F_TILES)]
+            if step + 1 < ROUNDS:
+                wi_grouped = regroup_wi(step + 1)
+            this_grouped = x_grouped
+            if step + 1 < steps:
+                x_grouped = transpose_x(step + 1)
+            if b == 1:
+                involution_windows(0, kr * windows_per_step, windows_per_step)
+            codes, scales = quantise_x(this_grouped)
+            if step + 1 < ROUNDS:
+                quantise_wi(step + 1, wi_grouped)
+            multiply(kr, acc, codes, scales)
+            if kr == ROUNDS - 1:
+                spread_xi(b, acc)
+        involution_windows(1, 0, HALVES * WINDOWS)

@@ -58,8 +58,8 @@ def tile_involution2d_pa_k_kernel(tc, x, Wi, bi, w_span, out):
         x_mx_pool = ctx.enter_context(tc.tile_pool(name="x_mx_pool", bufs=3))
         tail_pool = ctx.enter_context(tc.tile_pool(name="tail_pool", bufs=2))
         acc_pool = ctx.enter_context(tc.psum_pool(name="acc_pool", bufs=1))
-        xt_pool = ctx.enter_context(tc.psum_pool(name="xt_pool", bufs=4))
-        patch_pool = ctx.enter_context(tc.psum_pool(name="patch_pool", bufs=2))
+        work_pool = ctx.enter_context(tc.psum_pool(name="work_pool", bufs=6))
+        ctx.enter_context(tc.manual_schedule())
 
         ident = const.tile([P, P], F32)
         make_identity(nc, ident[:])
@@ -74,11 +74,13 @@ def tile_involution2d_pa_k_kernel(tc, x, Wi, bi, w_span, out):
         nc.vector.memset(bias_rows[:], 0.0)
         nc.scalar.dma_start(out=bias_rows[0:F_TILES, :], in_=bi.rearrange("(f c) -> f c", f=F_TILES))
         bias_rows32 = const.tile([P, P], F32)
-        nc.vector.tensor_copy(out=bias_rows32[:], in_=bias_rows[:])
-        patch = patch_pool.tile([P, WIN_BLOCKS * P], F32)
-        nc.tensor.transpose(patch[:, 0:P], bias_rows32[:], ident[:])
         bias_col = const.tile([P, F_TILES], F32)
-        nc.vector.tensor_copy(out=bias_col[:], in_=patch[:, 0:F_TILES])
+
+        def transpose_bias():
+            nc.vector.tensor_copy(out=bias_rows32[:], in_=bias_rows[:])
+            flipped = work_pool.tile([P, P], F32, tag="work")
+            nc.tensor.transpose(flipped[:], bias_rows32[:], ident[:])
+            nc.vector.tensor_copy(out=bias_col[:], in_=flipped[:, 0:F_TILES])
 
         xi_copies = []
         for b in range(IMAGES):
@@ -118,7 +120,7 @@ def tile_involution2d_pa_k_kernel(tc, x, Wi, bi, w_span, out):
             for g in range(ROUND):
                 dst = grouped[:, g, :, :].rearrange("p (c i) t -> p c t i", i=4)
                 src = raw[:, g, :, :].rearrange("p t (c i) -> p c t i", i=4)
-                if g % 2 == 0:
+                if g < ROUND - 1:
                     nc.vector.tensor_copy(out=dst, in_=src)
                 else:
                     nc.scalar.copy(out=dst, in_=src)
@@ -138,7 +140,7 @@ def tile_involution2d_pa_k_kernel(tc, x, Wi, bi, w_span, out):
             grouped_words = grouped[:].bitcast(F32)
             for g in range(ROUND):
                 first_word = ((step % CHUNK_ROUNDS) * ROUND + g) * PASS_WORDS
-                bank = xt_pool.tile([P, 2, IMG_PIX], F32)
+                bank = work_pool.tile([P, 2, IMG_PIX], F32, tag="work")
                 for u in range(2):
                     for h in range(HALVES):
                         nc.tensor.transpose(
@@ -206,7 +208,7 @@ def tile_involution2d_pa_k_kernel(tc, x, Wi, bi, w_span, out):
             xi = xi_copies[b]
             first_block = (WIN * wd) // P
             skip = WIN * wd - first_block * P
-            patch = patch_pool.tile([P, WIN_BLOCKS * P], F32)
+            patch = work_pool.tile([P, WIN_BLOCKS * P], F32, tag="work")
             for s in range(WIN_BLOCKS):
                 t, f = divmod(first_block + s, F_TILES)
                 i, j = divmod(t, 3)
@@ -249,9 +251,9 @@ def tile_involution2d_pa_k_kernel(tc, x, Wi, bi, w_span, out):
         windows_per_step = HALVES * WINDOWS // ROUNDS
         for step in range(LOAD_AHEAD):
             issue_loads(step)
-        wi_grouped = regroup_wi(0)
         x_grouped = transpose_x(0)
-        quantise_wi(0, wi_grouped)
+        wi_grouped = regroup_wi(0)
+        transpose_bias()
         acc = None
         for step in range(steps):
             b, kr = divmod(step, ROUNDS)
@@ -259,16 +261,15 @@ def tile_involution2d_pa_k_kernel(tc, x, Wi, bi, w_span, out):
                 issue_loads(step + LOAD_AHEAD)
             if kr == 0:
                 acc = [acc_pool.tile([P, IMG_PIX], F32, name="acc%d" % f) for f in range(F_TILES)]
-            if step + 1 < ROUNDS:
-                wi_grouped = regroup_wi(step + 1)
-            this_grouped = x_grouped
+            codes, scales = quantise_x(x_grouped)
+            if b == 0:
+                quantise_wi(kr, wi_grouped)
             if step + 1 < steps:
                 x_grouped = transpose_x(step + 1)
+            if step + 1 < ROUNDS:
+                wi_grouped = regroup_wi(step + 1)
             if b == 1:
                 involution_windows(0, kr * windows_per_step, windows_per_step)
-            codes, scales = quantise_x(this_grouped)
-            if step + 1 < ROUNDS:
-                quantise_wi(step + 1, wi_grouped)
             multiply(kr, acc, codes, scales)
             if kr == ROUNDS - 1:
                 spread_xi(b, acc)

@@ -28,6 +28,7 @@ ROUND = 4
 ROUNDS = PASSES // ROUND
 CHUNK_ROUNDS = 2
 CHUNK_K = CHUNK_ROUNDS * ROUND * K_PASS
+WI_LOAD_PASSES = 2
 LOAD_AHEAD = 4
 
 TAPS = 9
@@ -108,10 +109,12 @@ def tile_involution2d_pa_k_kernel(tc, x, Wi, bi, w_span, out):
                 x_chunks[chunk] = x_chunk
             if step < ROUNDS:
                 raw = wi_raw_pool.tile([P, ROUND, PACK, F_OUT], BF16)
-                nc.sync.dma_start(
-                    out=raw[:].rearrange("p g (u e) c -> p (g u) (e c)", u=2),
-                    in_=wi_rows[:, 2 * ROUND * step : 2 * ROUND * (step + 1), :],
-                )
+                for g in range(0, ROUND, WI_LOAD_PASSES):
+                    first_half_pass = 2 * (ROUND * step + g)
+                    nc.sync.dma_start(
+                        out=raw[:, g : g + WI_LOAD_PASSES, :, :].rearrange("p g (u e) c -> p (g u) (e c)", u=2),
+                        in_=wi_rows[:, first_half_pass : first_half_pass + 2 * WI_LOAD_PASSES, :],
+                    )
                 wi_raw[step] = raw
 
         def regroup_wi(kr):

@@ -28,7 +28,6 @@ ROUND = 4
 ROUNDS = PASSES // ROUND
 CHUNK_ROUNDS = 2
 CHUNK_K = CHUNK_ROUNDS * ROUND * K_PASS
-WI_LOAD_PASSES = 2
 LOAD_AHEAD = 4
 
 TAPS = 9
@@ -38,6 +37,8 @@ WIN_GROUPS = 2
 WIN = WIN_GROUPS * GROUP_CH * TAPS
 WINDOWS = GROUPS // WIN_GROUPS
 WIN_BLOCKS = 3
+IMG_WINDOWS = HALVES * WINDOWS
+STEP_WINDOWS = 3
 XI_LEFT = 32
 XI_WIDTH = 320
 
@@ -57,7 +58,9 @@ def tile_involution2d_pa_k_kernel(tc, x, Wi, bi, w_span, out):
         wi_grp_pool = ctx.enter_context(tc.tile_pool(name="wi_grp_pool", bufs=2))
         x_grp_pool = ctx.enter_context(tc.tile_pool(name="x_grp_pool", bufs=3))
         x_mx_pool = ctx.enter_context(tc.tile_pool(name="x_mx_pool", bufs=3))
-        tail_pool = ctx.enter_context(tc.tile_pool(name="tail_pool", bufs=2))
+        products_pool = ctx.enter_context(tc.tile_pool(name="products_pool", bufs=1))
+        result_pool = ctx.enter_context(tc.tile_pool(name="result_pool", bufs=2))
+        patch_sb_pool = ctx.enter_context(tc.tile_pool(name="patch_sb_pool", bufs=3))
         acc_pool = ctx.enter_context(tc.psum_pool(name="acc_pool", bufs=1))
         work_pool = ctx.enter_context(tc.psum_pool(name="work_pool", bufs=6))
         ctx.enter_context(tc.manual_schedule())
@@ -73,9 +76,10 @@ def tile_involution2d_pa_k_kernel(tc, x, Wi, bi, w_span, out):
 
         bias_rows = const.tile([P, P], BF16)
         nc.vector.memset(bias_rows[:], 0.0)
+        bias_col = const.tile([P, F_TILES], F32)
+        nc.scalar.activation(out=bias_col[:], in_=bias_rows[:, 0:F_TILES], func=ACT.Identity)
         nc.scalar.dma_start(out=bias_rows[0:F_TILES, :], in_=bi.rearrange("(f c) -> f c", f=F_TILES))
         bias_rows32 = const.tile([P, P], F32)
-        bias_col = const.tile([P, F_TILES], F32)
 
         def transpose_bias():
             nc.vector.tensor_copy(out=bias_rows32[:], in_=bias_rows[:])
@@ -109,12 +113,10 @@ def tile_involution2d_pa_k_kernel(tc, x, Wi, bi, w_span, out):
                 x_chunks[chunk] = x_chunk
             if step < ROUNDS:
                 raw = wi_raw_pool.tile([P, ROUND, PACK, F_OUT], BF16)
-                for g in range(0, ROUND, WI_LOAD_PASSES):
-                    first_half_pass = 2 * (ROUND * step + g)
-                    nc.sync.dma_start(
-                        out=raw[:, g : g + WI_LOAD_PASSES, :, :].rearrange("p g (u e) c -> p (g u) (e c)", u=2),
-                        in_=wi_rows[:, first_half_pass : first_half_pass + 2 * WI_LOAD_PASSES, :],
-                    )
+                nc.sync.dma_start(
+                    out=raw[:].rearrange("p g (u e) c -> p (g u) (e c)", u=2),
+                    in_=wi_rows[:, 2 * ROUND * step : 2 * ROUND * (step + 1), :],
+                )
                 wi_raw[step] = raw
 
         def regroup_wi(kr):
@@ -207,8 +209,9 @@ def tile_involution2d_pa_k_kernel(tc, x, Wi, bi, w_span, out):
                             op0=ALU.add,
                         )
 
-        def weigh_window(b, h, wd, products):
+        def weigh_window(b, e, products):
             xi = xi_copies[b]
+            h, wd = divmod(e, WINDOWS)
             first_block = (WIN * wd) // P
             skip = WIN * wd - first_block * P
             patch = work_pool.tile([P, WIN_BLOCKS * P], F32, tag="work")
@@ -217,47 +220,54 @@ def tile_involution2d_pa_k_kernel(tc, x, Wi, bi, w_span, out):
                 i, j = divmod(t, 3)
                 start = XI_LEFT + h * P + (i - 1) * SIDE
                 nc.tensor.transpose(patch[:, s * P : (s + 1) * P], xi[:, j, f, start : start + P], ident[:])
-            weights = w_sb[:, b * HALVES + h, WIN_GROUPS * TAPS * wd : WIN_GROUPS * TAPS * (wd + 1)]
-            nc.vector.tensor_tensor(
-                out=products[:, WIN * wd : WIN * (wd + 1)].rearrange("p (g c m) -> p g c m", g=WIN_GROUPS, m=TAPS),
-                in0=patch[:, skip : skip + WIN].rearrange("p (g c m) -> p g c m", g=WIN_GROUPS, m=TAPS),
-                in1=weights.rearrange("p (g m) -> p g m", m=TAPS)
+            weights = (
+                w_sb[:, b * HALVES + h, WIN_GROUPS * TAPS * wd : WIN_GROUPS * TAPS * (wd + 1)]
+                .rearrange("p (g m) -> p g m", m=TAPS)
                 .unsqueeze(2)
-                .to_broadcast([P, WIN_GROUPS, GROUP_CH, TAPS]),
-                op=ALU.mult,
+                .to_broadcast([P, WIN_GROUPS, GROUP_CH, TAPS])
             )
+            weighed = products[:, WIN * e : WIN * (e + 1)].rearrange("p (g c m) -> p g c m", g=WIN_GROUPS, m=TAPS)
+            if e % 3 != 1:
+                nc.vector.tensor_tensor(
+                    out=weighed,
+                    in0=patch[:, skip : skip + WIN].rearrange("p (g c m) -> p g c m", g=WIN_GROUPS, m=TAPS),
+                    in1=weights,
+                    op=ALU.mult,
+                )
+            else:
+                patch_sb = patch_sb_pool.tile([P, WIN], F32)
+                nc.scalar.copy(out=patch_sb[:], in_=patch[:, skip : skip + WIN])
+                nc.gpsimd.tensor_tensor(
+                    out=weighed,
+                    in0=patch_sb[:].rearrange("p (g c m) -> p g c m", g=WIN_GROUPS, m=TAPS),
+                    in1=weights,
+                    op=ALU.mult,
+                )
 
-        def sum_and_store(b, h, products):
-            result = tail_pool.tile([P, F_OUT], F32)
+        def sum_windows(b, first, count, products, result):
+            outputs = WIN // TAPS
             nc.vector.tensor_reduce(
-                out=result[:],
-                in_=products[:].rearrange("p (o m) -> p o m", m=TAPS),
+                out=result[:, outputs * first : outputs * (first + count)],
+                in_=products[:, WIN * first : WIN * (first + count)].rearrange("p (o m) -> p o m", m=TAPS),
                 axis=AXIS.X,
                 op=ALU.add,
             )
-            first_pixel = (b * HALVES + h) * P
-            nc.sync.dma_start(out=out_rows[first_pixel : first_pixel + P, :], in_=result[:])
-
-        products_of = {}
-
-        def involution_windows(b, first, count):
-            for e in range(first, first + count):
-                h, wd = divmod(e, WINDOWS)
-                if wd == 0:
-                    products = tail_pool.tile([P, F_OUT * TAPS], F32)
-                    products_of[h] = products
-                weigh_window(b, h, wd, products_of[h])
-                if wd == WINDOWS - 1:
-                    sum_and_store(b, h, products_of[h])
+            for h in range(HALVES):
+                if first < WINDOWS * (h + 1) <= first + count:
+                    first_pixel = (b * HALVES + h) * P
+                    nc.sync.dma_start(
+                        out=out_rows[first_pixel : first_pixel + P, :], in_=result[:, h * F_OUT : (h + 1) * F_OUT]
+                    )
 
         steps = IMAGES * ROUNDS
-        windows_per_step = HALVES * WINDOWS // ROUNDS
         for step in range(LOAD_AHEAD):
             issue_loads(step)
         x_grouped = transpose_x(0)
         wi_grouped = regroup_wi(0)
         transpose_bias()
         acc = None
+        products = None
+        result = None
         for step in range(steps):
             b, kr = divmod(step, ROUNDS)
             if step + LOAD_AHEAD < steps:
@@ -272,8 +282,20 @@ def tile_involution2d_pa_k_kernel(tc, x, Wi, bi, w_span, out):
             if step + 1 < ROUNDS:
                 wi_grouped = regroup_wi(step + 1)
             if b == 1:
-                involution_windows(0, kr * windows_per_step, windows_per_step)
+                if kr == 0:
+                    products = products_pool.tile([P, IMG_WINDOWS * WIN], F32)
+                    result = result_pool.tile([P, HALVES * F_OUT], F32)
+                summed = (kr - 1) * STEP_WINDOWS
+                if 0 <= summed < IMG_WINDOWS:
+                    sum_windows(0, summed, min(STEP_WINDOWS, IMG_WINDOWS - summed), products, result)
+                for e in range(kr * STEP_WINDOWS, min((kr + 1) * STEP_WINDOWS, IMG_WINDOWS)):
+                    weigh_window(0, e, products)
             multiply(kr, acc, codes, scales)
             if kr == ROUNDS - 1:
                 spread_xi(b, acc)
-        involution_windows(1, 0, HALVES * WINDOWS)
+        products = products_pool.tile([P, IMG_WINDOWS * WIN], F32)
+        result = result_pool.tile([P, HALVES * F_OUT], F32)
+        for e in range(IMG_WINDOWS):
+            weigh_window(1, e, products)
+        for h in range(HALVES):
+            sum_windows(1, h * WINDOWS, WINDOWS, products, result)

from contextlib import ExitStack

import concourse.mybir as mybir
from concourse.masks import make_identity

F32 = mybir.dt.float32
BF16 = mybir.dt.bfloat16
U32 = mybir.dt.uint32
U8 = mybir.dt.uint8
FP8X4 = mybir.dt.float8_e4m3fn_x4
ALU = mybir.AluOpType
ACT = mybir.ActivationFunctionType
AXIS = mybir.AxisListType

P = 128
IMAGES = 2
SIDE = 16
IMG_PIX = SIDE * SIDE
HALVES = IMG_PIX // P
C_IN = 16384
F_OUT = 256
F_TILES = F_OUT // P
PACK = 4
K_PASS = P * PACK
PASS_WORDS = K_PASS // 2
PASSES = C_IN // K_PASS
ROUND = 4
ROUNDS = PASSES // ROUND
CHUNK_ROUNDS = 2
CHUNK_K = CHUNK_ROUNDS * ROUND * K_PASS
LOAD_AHEAD = 4

TAPS = 9
GROUPS = 16
GROUP_CH = F_OUT // GROUPS
WIN_GROUPS = 2
WIN = WIN_GROUPS * GROUP_CH * TAPS
WINDOWS = GROUPS // WIN_GROUPS
WIN_BLOCKS = 3
IMG_WINDOWS = HALVES * WINDOWS
STEP_WINDOWS = 3
XI_LEFT = 32
XI_WIDTH = 320

FLOPS = 2 * IMAGES * IMG_PIX * C_IN * F_OUT


def tile_involution2d_pa_k_kernel(tc, x, Wi, bi, w_span, out):
    nc = tc.nc
    x_rows = x.rearrange("b u v k -> (b u v) k")
    out_rows = out.rearrange("b u v o -> (b u v) o")
    wi_rows = Wi.rearrange("(a p e) c -> p a (e c)", p=P, e=2)

    with ExitStack() as ctx:
        const = ctx.enter_context(tc.tile_pool(name="const", bufs=1))
        x_pool = ctx.enter_context(tc.tile_pool(name="x_pool", bufs=3))
        wi_raw_pool = ctx.enter_context(tc.tile_pool(name="wi_raw_pool", bufs=LOAD_AHEAD + 1))
        wi_grp_pool = ctx.enter_context(tc.tile_pool(name="wi_grp_pool", bufs=2))
        x_grp_pool = ctx.enter_context(tc.tile_pool(name="x_grp_pool", bufs=3))
        x_mx_pool = ctx.enter_context(tc.tile_pool(name="x_mx_pool", bufs=3))
        products_pool = ctx.enter_context(tc.tile_pool(name="products_pool", bufs=1))
        result_pool = ctx.enter_context(tc.tile_pool(name="result_pool", bufs=2))
        patch_sb_pool = ctx.enter_context(tc.tile_pool(name="patch_sb_pool", bufs=3))
        acc_pool = ctx.enter_context(tc.psum_pool(name="acc_pool", bufs=1))
        work_pool = ctx.enter_context(tc.psum_pool(name="work_pool", bufs=6))
        ctx.enter_context(tc.manual_schedule())

        ident = const.tile([P, P], F32)
        make_identity(nc, ident[:])

        w_sb = const.tile([P, IMAGES * HALVES, GROUPS * TAPS], BF16)
        nc.scalar.dma_start(
            out=w_sb[:],
            in_=w_span.rearrange("b u v q -> (b u v) q").rearrange("(r p) q -> p r q", p=P),
        )

        bias_rows = const.tile([P, P], BF16)
        nc.vector.memset(bias_rows[:], 0.0)
        bias_col = const.tile([P, F_TILES], F32)
        nc.scalar.activation(out=bias_col[:], in_=bias_rows[:, 0:F_TILES], func=ACT.Identity)
        nc.scalar.dma_start(out=bias_rows[0:F_TILES, :], in_=bi.rearrange("(f c) -> f c", f=F_TILES))
        bias_rows32 = const.tile([P, P], F32)

        def transpose_bias():
            nc.vector.tensor_copy(out=bias_rows32[:], in_=bias_rows[:])
            flipped = work_pool.tile([P, P], F32, tag="work")
            nc.tensor.transpose(flipped[:], bias_rows32[:], ident[:])
            nc.vector.tensor_copy(out=bias_col[:], in_=flipped[:, 0:F_TILES])

        xi_copies = []
        for b in range(IMAGES):
            xi = const.tile([P, 3, F_TILES, XI_WIDTH], F32, name="xi%d" % b)
            nc.vector.memset(xi[:], 0.0)
            xi_copies.append(xi)

        wi_codes = const.tile([P, PASSES * F_OUT], U32, align_bytes=64)
        wi_scales = const.tile([P, PASSES * F_OUT], U8, align_bytes=64)

        wi_raw = {}
        x_chunks = {}

        def issue_loads(step):
            if step % CHUNK_ROUNDS == 0:
                chunk = step // CHUNK_ROUNDS
                b, part = divmod(chunk, ROUNDS // CHUNK_ROUNDS)
                x_chunk = x_pool.tile([P, HALVES, CHUNK_K], BF16)
                for h in range(HALVES):
                    first_pixel = (b * HALVES + h) * P
                    nc.sync.dma_start(
                        out=x_chunk[:, h, :],
                        in_=x_rows[first_pixel : first_pixel + P, part * CHUNK_K : (part + 1) * CHUNK_K],
                    )
                x_chunks[chunk] = x_chunk
            if step < ROUNDS:
                raw = wi_raw_pool.tile([P, ROUND, PACK, F_OUT], BF16)
                nc.sync.dma_start(
                    out=raw[:].rearrange("p g (u e) c -> p (g u) (e c)", u=2),
                    in_=wi_rows[:, 2 * ROUND * step : 2 * ROUND * (step + 1), :],
                )
                wi_raw[step] = raw

        def regroup_wi(kr):
            raw = wi_raw[kr]
            grouped = wi_grp_pool.tile([P, ROUND, F_OUT, PACK], BF16, align_bytes=64)
            for g in range(ROUND):
                dst = grouped[:, g, :, :].rearrange("p (c i) t -> p c t i", i=4)
                src = raw[:, g, :, :].rearrange("p t (c i) -> p c t i", i=4)
                if g < ROUND - 1:
                    nc.vector.tensor_copy(out=dst, in_=src)
                else:
                    nc.scalar.copy(out=dst, in_=src)
            return grouped

        def quantise_wi(kr, grouped):
            cols = slice(kr * ROUND * F_OUT, (kr + 1) * ROUND * F_OUT)
            nc.vector.quantize_mx(
                out=wi_codes[:, cols].bitcast(FP8X4),
                scales=wi_scales[:, cols],
                in_=grouped[:].rearrange("p g c t -> p (g c t)"),
            )

        def transpose_x(step):
            x_chunk = x_chunks[step // CHUNK_ROUNDS]
            grouped = x_grp_pool.tile([P, ROUND * IMG_PIX * PACK], BF16, align_bytes=64)
            grouped_words = grouped[:].bitcast(F32)
            for g in range(ROUND):
                first_word = ((step % CHUNK_ROUNDS) * ROUND + g) * PASS_WORDS
                bank = work_pool.tile([P, 2, IMG_PIX], F32, tag="work")
                for u in range(2):
                    for h in range(HALVES):
                        nc.tensor.transpose(
                            bank[:, u, h * P : (h + 1) * P],
                            x_chunk[:, h, :].bitcast(F32)[:, first_word + u * P : first_word + (u + 1) * P],
                            ident[:],
                        )
                nc.scalar.copy(
                    out=grouped_words[:, g * 2 * IMG_PIX : (g + 1) * 2 * IMG_PIX].rearrange(
                        "p (r u) -> p r u", u=2
                    ),
                    in_=bank[:].rearrange("p u r -> p r u"),
                )
            return grouped

        def quantise_x(grouped):
            codes = x_mx_pool.tile([P, ROUND * IMG_PIX], U32, align_bytes=64)
            scales = x_mx_pool.tile([P, ROUND * IMG_PIX], U8, align_bytes=64)
            nc.vector.quantize_mx(out=codes[:].bitcast(FP8X4), scales=scales[:], in_=grouped[:])
            return codes, scales

        def multiply(kr, acc, codes, scales):
            for g in range(ROUND):
                k_pass = kr * ROUND + g
                pixels = slice(g * IMG_PIX, (g + 1) * IMG_PIX)
                for f in range(F_TILES):
                    columns = slice(k_pass * F_OUT + f * P, k_pass * F_OUT + (f + 1) * P)
                    nc.tensor.matmul_mx(
                        out=acc[f][:],
                        lhsT=wi_codes[:, columns].bitcast(FP8X4),
                        lhsT_scale=wi_scales[:, columns],
                        rhs=codes[:, pixels].bitcast(FP8X4),
                        rhs_scale=scales[:, pixels],
                        start=(k_pass == 0),
                        stop=(k_pass == PASSES - 1),
                    )

        def spread_xi(b, acc):
            xi = xi_copies[b]
            for f in range(F_TILES):
                image = acc[f][:].rearrange("p (u v) -> p u v", v=SIDE)
                for j in range(3):
                    v_lo = max(0, j - 1)
                    v_hi = min(SIDE, SIDE - 1 + j)
                    first = XI_LEFT - (j - 1)
                    dst = xi[:, j, f, first : first + IMG_PIX].rearrange("p (u v) -> p u v", v=SIDE)
                    if f == 0:
                        nc.scalar.activation(
                            out=dst[:, :, v_lo:v_hi],
                            in_=image[:, :, v_lo:v_hi],
                            func=ACT.Identity,
                            bias=bias_col[:, f : f + 1],
                            scale=1.0,
                        )
                    else:
                        nc.vector.tensor_scalar(
                            out=dst[:, :, v_lo:v_hi],
                            in0=image[:, :, v_lo:v_hi],
                            scalar1=bias_col[:, f : f + 1],
                            scalar2=None,
                            op0=ALU.add,
                        )

        def weigh_window(b, e, products):
            xi = xi_copies[b]
            h, wd = divmod(e, WINDOWS)
            first_block = (WIN * wd) // P
            skip = WIN * wd - first_block * P
            patch = work_pool.tile([P, WIN_BLOCKS * P], F32, tag="work")
            for s in range(WIN_BLOCKS):
                t, f = divmod(first_block + s, F_TILES)
                i, j = divmod(t, 3)
                start = XI_LEFT + h * P + (i - 1) * SIDE
                nc.tensor.transpose(patch[:, s * P : (s + 1) * P], xi[:, j, f, start : start + P], ident[:])
            weights = (
                w_sb[:, b * HALVES + h, WIN_GROUPS * TAPS * wd : WIN_GROUPS * TAPS * (wd + 1)]
                .rearrange("p (g m) -> p g m", m=TAPS)
                .unsqueeze(2)
                .to_broadcast([P, WIN_GROUPS, GROUP_CH, TAPS])
            )
            weighed = products[:, WIN * e : WIN * (e + 1)].rearrange("p (g c m) -> p g c m", g=WIN_GROUPS, m=TAPS)
            if e % 3 != 1:
                nc.vector.tensor_tensor(
                    out=weighed,
                    in0=patch[:, skip : skip + WIN].rearrange("p (g c m) -> p g c m", g=WIN_GROUPS, m=TAPS),
                    in1=weights,
                    op=ALU.mult,
                )
            else:
                patch_sb = patch_sb_pool.tile([P, WIN], F32)
                nc.scalar.copy(out=patch_sb[:], in_=patch[:, skip : skip + WIN])
                nc.gpsimd.tensor_tensor(
                    out=weighed,
                    in0=patch_sb[:].rearrange("p (g c m) -> p g c m", g=WIN_GROUPS, m=TAPS),
                    in1=weights,
                    op=ALU.mult,
                )

        def sum_windows(b, first, count, products, result):
            outputs = WIN // TAPS
            nc.vector.tensor_reduce(
                out=result[:, outputs * first : outputs * (first + count)],
                in_=products[:, WIN * first : WIN * (first + count)].rearrange("p (o m) -> p o m", m=TAPS),
                axis=AXIS.X,
                op=ALU.add,
            )
            for h in range(HALVES):
                if first < WINDOWS * (h + 1) <= first + count:
                    first_pixel = (b * HALVES + h) * P
                    nc.sync.dma_start(
                        out=out_rows[first_pixel : first_pixel + P, :], in_=result[:, h * F_OUT : (h + 1) * F_OUT]
                    )

        steps = IMAGES * ROUNDS
        for step in range(LOAD_AHEAD):
            issue_loads(step)
        x_grouped = transpose_x(0)
        wi_grouped = regroup_wi(0)
        transpose_bias()
        acc = None
        products = None
        result = None
        for step in range(steps):
            b, kr = divmod(step, ROUNDS)
            if step + LOAD_AHEAD < steps:
                issue_loads(step + LOAD_AHEAD)
            if kr == 0:
                acc = [acc_pool.tile([P, IMG_PIX], F32, name="acc%d" % f) for f in range(F_TILES)]
            codes, scales = quantise_x(x_grouped)
            if b == 0:
                quantise_wi(kr, wi_grouped)
            if step + 1 < steps:
                x_grouped = transpose_x(step + 1)
            if step + 1 < ROUNDS:
                wi_grouped = regroup_wi(step + 1)
            if b == 1:
                if kr == 0:
                    products = products_pool.tile([P, IMG_WINDOWS * WIN], F32)
                    result = result_pool.tile([P, HALVES * F_OUT], F32)
                summed = (kr - 1) * STEP_WINDOWS
                if 0 <= summed < IMG_WINDOWS:
                    sum_windows(0, summed, min(STEP_WINDOWS, IMG_WINDOWS - summed), products, result)
                for e in range(kr * STEP_WINDOWS, min((kr + 1) * STEP_WINDOWS, IMG_WINDOWS)):
                    weigh_window(0, e, products)
            multiply(kr, acc, codes, scales)
            if kr == ROUNDS - 1:
                spread_xi(b, acc)
        products = products_pool.tile([P, IMG_WINDOWS * WIN], F32)
        result = result_pool.tile([P, HALVES * F_OUT], F32)
        for e in range(IMG_WINDOWS):
            weigh_window(1, e, products)
        for h in range(HALVES):
            sum_windows(1, h * WINDOWS, WINDOWS, products, result)
